import numpy as np
import ml_dtypes

BF16 = ml_dtypes.bfloat16


def bf(x):
    return np.asarray(x, np.float32).astype(BF16)


def f32(x):
    return np.asarray(x, np.float32)


def f64(x):
    return np.asarray(x).astype(np.float64)


def striped(idx):
    return np.tile(idx.reshape(-1, 16).T, (8, 1))


C, S, N, O, GS = 512, 4096, 2048, 256, 128
NG = N // GS
LEVELS, STEP, ZMAX, SPREAD = 16, 16, 255.0, 100.0


def setup_inputs():
    return {
        "x": f32(np.random.standard_normal((C, S))),
        "code": bf(STEP * np.random.choice(LEVELS, size=(N, O))),
        "scale": f32((0.5 + np.random.random((NG, O))) / (SPREAD * np.sqrt(N))),
        "zero": f32(ZMAX * np.random.random((NG, O))),
        "bias": f32(np.random.standard_normal((1, O))),
        "offs": striped(np.random.permutation(S)[:N]),
    }


def reference(x, code, scale, zero, bias, offs):
    idx = offs[:16].T.reshape(-1)
    w = np.repeat(f64(scale), GS, axis=0) * (f64(code) - np.repeat(f64(zero), GS, axis=0))
    return f64(x)[:, idx] @ w + f64(bias)

@@ -1,0 +1,97 @@
+import concourse.masks as masks
+import concourse.mybir as mybir
+
+F32 = mybir.dt.float32
+BF16 = mybir.dt.bfloat16
+U16 = mybir.dt.uint16
+
+P = 128
+TOKENS = 512
+FEATURES = 4096
+PICKED = 2048
+OUT = 256
+GROUP = 128
+GROUPS = PICKED // GROUP
+BLOCKS = TOKENS // P
+KTILES = PICKED // P
+SHARE = P // GROUPS
+BANK = 512
+FLIPS = BANK // P
+
+FLOPS = 2 * TOKENS * PICKED * OUT
+
+
+def tile_fakematryoshkalinear_kernel(tc, x, code, scale, zero, bias, offs, out):
+    nc = tc.nc
+    copy = mybir.ActivationFunctionType.Copy
+    subtract, mult, add = mybir.AluOpType.subtract, mybir.AluOpType.mult, mybir.AluOpType.add
+
+    with (
+        tc.tile_pool(name="held", bufs=1) as held,
+        tc.tile_pool(name="windows", bufs=BLOCKS) as windows,
+        tc.tile_pool(name="work", bufs=2) as work,
+        tc.psum_pool(name="flip_banks", bufs=4) as flip_banks,
+        tc.psum_pool(name="sum_banks", bufs=2) as sum_banks,
+    ):
+        offsets = held.tile([P, PICKED // 16], U16, name="offsets")
+        nc.sync.dma_start(offsets[:], offs)
+
+        code_sb = held.tile([P, KTILES, OUT], BF16, name="code_sb")
+        nc.sync.dma_start(code_sb[:], code.rearrange("(p k) o -> p k o", k=KTILES))
+
+        x_blocks = []
+        for b in range(BLOCKS):
+            x_block = windows.tile([P, FEATURES], F32, name="x_block")
+            nc.sync.dma_start(x_block[:], x[b * P : (b + 1) * P, :])
+            x_blocks.append(x_block)
+
+        scale_rows = held.tile([P, OUT], F32, name="scale_rows")
+        zero_rows = held.tile([P, OUT], F32, name="zero_rows")
+        bias_rows = held.tile([P, OUT], F32, name="bias_rows")
+        for g in range(GROUPS):
+            rows = slice(g * SHARE, (g + 1) * SHARE)
+            nc.scalar.dma_start(zero_rows[rows, :], zero[g, :].partition_broadcast(SHARE))
+            nc.scalar.dma_start(scale_rows[rows, :], scale[g, :].partition_broadcast(SHARE))
+        nc.scalar.dma_start(bias_rows[:], bias[0, :].partition_broadcast(P))
+
+        identity = held.tile([P, P], F32, name="identity")
+        masks.make_identity(nc, identity[:])
+
+        w = held.tile([P, KTILES, OUT], BF16, name="w")
+        for c in range(KTILES // FLIPS):
+            tiles = slice(c * FLIPS, (c + 1) * FLIPS)
+            shifted = work.tile([P, FLIPS, OUT], F32, name="shifted")
+            nc.vector.tensor_tensor(
+                shifted[:],
+                code_sb[:, tiles, :],
+                zero_rows[:].unsqueeze(1).to_broadcast([P, FLIPS, OUT]),
+                subtract,
+            )
+            nc.vector.tensor_tensor(
+                w[:, tiles, :],
+                shifted[:],
+                scale_rows[:].unsqueeze(1).to_broadcast([P, FLIPS, OUT]),
+                mult,
+            )
+
+        for b in range(BLOCKS):
+            picked = work.tile([P, PICKED], F32, name="picked")
+            nc.scalar.activation(picked[:], x_blocks[b][:].indirect(offsets[:]), copy)
+
+            by_tile = picked[:].rearrange("t (p k) -> t k p", k=KTILES)
+            picked_t = work.tile([P, KTILES, P], BF16, name="picked_t")
+            for c in range(KTILES // FLIPS):
+                flipped = flip_banks.tile([P, FLIPS, P], F32, name="flipped")
+                for i in range(FLIPS):
+                    nc.tensor.transpose(flipped[:, i, :], by_tile[:, c * FLIPS + i, :], identity[:])
+                nc.vector.tensor_copy(picked_t[:, c * FLIPS : (c + 1) * FLIPS, :], flipped[:])
+
+            sums = sum_banks.tile([P, OUT], F32, name="sums")
+            for k in range(KTILES):
+                nc.tensor.matmul(
+                    sums[:], picked_t[:, k, :], w[:, k, :], start=(k == 0), stop=(k == KTILES - 1)
+                )
+
+            result = work.tile([P, OUT], F32, name="result")
+            nc.vector.tensor_tensor(result[:], sums[:], bias_rows[:], add)
+            nc.sync.dma_start(out[b * P : (b + 1) * P, :], result[:])

@@ -13,10 +13,10 @@ OUT = 256
 GROUP = 128
 GROUPS = PICKED // GROUP
 BLOCKS = TOKENS // P
-KTILES = PICKED // P
-SHARE = P // GROUPS
-BANK = 512
-FLIPS = BANK // P
+PIECE = 512
+PIECES = PICKED // PIECE
+KTILES = PIECE // P
+SHARE = P * GROUP // PIECE
 
 FLOPS = 2 * TOKENS * PICKED * OUT
 
@@ -24,20 +24,28 @@ FLOPS = 2 * TOKENS * PICKED * OUT
 def tile_fakematryoshkalinear_kernel(tc, x, code, scale, zero, bias, offs, out):
     nc = tc.nc
     copy = mybir.ActivationFunctionType.Copy
-    subtract, mult, add = mybir.AluOpType.subtract, mybir.AluOpType.mult, mybir.AluOpType.add
+    alu = mybir.AluOpType
 
     with (
         tc.tile_pool(name="held", bufs=1) as held,
         tc.tile_pool(name="windows", bufs=BLOCKS) as windows,
         tc.tile_pool(name="work", bufs=2) as work,
-        tc.psum_pool(name="flip_banks", bufs=4) as flip_banks,
+        tc.tile_pool(name="ring", bufs=6) as ring,
+        tc.psum_pool(name="spread_banks", bufs=PIECES) as spread_banks,
+        tc.psum_pool(name="flip_banks", bufs=2) as flip_banks,
         tc.psum_pool(name="sum_banks", bufs=2) as sum_banks,
     ):
+        scale_zero = held.tile([GROUPS, 2 * OUT], F32, name="scale_zero")
+        nc.scalar.dma_start(scale_zero[:, 0:OUT], scale)
+        nc.scalar.dma_start(scale_zero[:, OUT : 2 * OUT], zero)
+        bias_rows = held.tile([P, OUT], F32, name="bias_rows")
+        nc.scalar.dma_start(bias_rows[:], bias[0, :].partition_broadcast(P))
+
         offsets = held.tile([P, PICKED // 16], U16, name="offsets")
         nc.sync.dma_start(offsets[:], offs)
 
-        code_sb = held.tile([P, KTILES, OUT], BF16, name="code_sb")
-        nc.sync.dma_start(code_sb[:], code.rearrange("(p k) o -> p k o", k=KTILES))
+        code_sb = held.tile([P, PIECES, KTILES, OUT], BF16, name="code_sb")
+        nc.sync.dma_start(code_sb[:], code.rearrange("(h p k) o -> p h k o", h=PIECES, k=KTILES))
 
         x_blocks = []
         for b in range(BLOCKS):
@@ -45,53 +53,68 @@ def tile_fakematryoshkalinear_kernel(tc, x, code, scale, zero, bias, offs, out):
             nc.sync.dma_start(x_block[:], x[b * P : (b + 1) * P, :])
             x_blocks.append(x_block)
 
-        scale_rows = held.tile([P, OUT], F32, name="scale_rows")
-        zero_rows = held.tile([P, OUT], F32, name="zero_rows")
-        bias_rows = held.tile([P, OUT], F32, name="bias_rows")
-        for g in range(GROUPS):
-            rows = slice(g * SHARE, (g + 1) * SHARE)
-            nc.scalar.dma_start(zero_rows[rows, :], zero[g, :].partition_broadcast(SHARE))
-            nc.scalar.dma_start(scale_rows[rows, :], scale[g, :].partition_broadcast(SHARE))
-        nc.scalar.dma_start(bias_rows[:], bias[0, :].partition_broadcast(P))
-
         identity = held.tile([P, P], F32, name="identity")
         masks.make_identity(nc, identity[:])
 
-        w = held.tile([P, KTILES, OUT], BF16, name="w")
-        for c in range(KTILES // FLIPS):
-            tiles = slice(c * FLIPS, (c + 1) * FLIPS)
-            shifted = work.tile([P, FLIPS, OUT], F32, name="shifted")
+        selector = held.tile([GROUPS, PIECES * P], F32, name="selector")
+        nc.gpsimd.memset(selector[:], 1.0)
+        nc.gpsimd.affine_select(
+            out=selector[:], in_=selector[:], compare_op=alu.is_ge, fill=0.0,
+            base=0, pattern=[[1, PIECES * P]], channel_multiplier=-SHARE,
+        )
+        nc.gpsimd.affine_select(
+            out=selector[:], in_=selector[:], compare_op=alu.is_ge, fill=0.0,
+            base=SHARE - 1, pattern=[[-1, PIECES * P]], channel_multiplier=SHARE,
+        )
+
+        w = held.tile([P, PIECES, KTILES, OUT], BF16, name="w")
+        for h in range(PIECES):
+            spread = spread_banks.tile([P, 2 * OUT], F32, name="spread")
+            nc.tensor.matmul(spread[:], selector[:, h * P : (h + 1) * P], scale_zero[:], start=True, stop=True)
+            shifted = work.tile([P, KTILES, OUT], F32, name="shifted")
             nc.vector.tensor_tensor(
                 shifted[:],
-                code_sb[:, tiles, :],
-                zero_rows[:].unsqueeze(1).to_broadcast([P, FLIPS, OUT]),
-                subtract,
+                code_sb[:, h, :, :],
+                spread[:, OUT : 2 * OUT].unsqueeze(1).to_broadcast([P, KTILES, OUT]),
+                alu.subtract,
             )
             nc.vector.tensor_tensor(
-                w[:, tiles, :],
+                w[:, h, :, :],
                 shifted[:],
-                scale_rows[:].unsqueeze(1).to_broadcast([P, FLIPS, OUT]),
-                mult,
+                spread[:, 0:OUT].unsqueeze(1).to_broadcast([P, KTILES, OUT]),
+                alu.mult,
             )
 
-        for b in range(BLOCKS):
-            picked = work.tile([P, PICKED], F32, name="picked")
-            nc.scalar.activation(picked[:], x_blocks[b][:].indirect(offsets[:]), copy)
+        flipped_pieces = []
+        sums = None
+        for step in range(BLOCKS * PIECES + 1):
+            if step < BLOCKS * PIECES:
+                b, h = divmod(step, PIECES)
+                picked = ring.tile([P, PIECE], F32, name="picked")
+                piece_offsets = offsets[:, h * (PIECE // 16) : (h + 1) * (PIECE // 16)]
+                nc.scalar.activation(picked[:], x_blocks[b][:].indirect(piece_offsets), copy)
 
-            by_tile = picked[:].rearrange("t (p k) -> t k p", k=KTILES)
-            picked_t = work.tile([P, KTILES, P], BF16, name="picked_t")
-            for c in range(KTILES // FLIPS):
-                flipped = flip_banks.tile([P, FLIPS, P], F32, name="flipped")
-                for i in range(FLIPS):
-                    nc.tensor.transpose(flipped[:, i, :], by_tile[:, c * FLIPS + i, :], identity[:])
-                nc.vector.tensor_copy(picked_t[:, c * FLIPS : (c + 1) * FLIPS, :], flipped[:])
+                by_tile = picked[:].rearrange("t (p k) -> t k p", k=KTILES)
+                flipped = flip_banks.tile([P, KTILES, P], F32, name="flipped")
+                for k in range(KTILES):
+                    nc.tensor.transpose(flipped[:, k, :], by_tile[:, k, :], identity[:])
+                picked_t = ring.tile([P, KTILES, P], BF16, name="picked_t")
+                nc.vector.tensor_copy(picked_t[:], flipped[:])
+                flipped_pieces.append(picked_t)
 
-            sums = sum_banks.tile([P, OUT], F32, name="sums")
-            for k in range(KTILES):
-                nc.tensor.matmul(
-                    sums[:], picked_t[:, k, :], w[:, k, :], start=(k == 0), stop=(k == KTILES - 1)
-                )
-
-            result = work.tile([P, OUT], F32, name="result")
-            nc.vector.tensor_tensor(result[:], sums[:], bias_rows[:], add)
-            nc.sync.dma_start(out[b * P : (b + 1) * P, :], result[:])
+            if step > 0:
+                b, h = divmod(step - 1, PIECES)
+                if h == 0:
+                    sums = sum_banks.tile([P, OUT], F32, name="sums")
+                for k in range(KTILES):
+                    nc.tensor.matmul(
+                        sums[:],
+                        flipped_pieces[step - 1][:, k, :],
+                        w[:, h, k, :],
+                        start=(h == 0 and k == 0),
+                        stop=(h == PIECES - 1 and k == KTILES - 1),
+                    )
+                if h == PIECES - 1:
+                    result = work.tile([P, OUT], F32, name="result")
+                    nc.vector.tensor_tensor(result[:], sums[:], bias_rows[:], alu.add)
+                    nc.sync.dma_start(out[b * P : (b + 1) * P, :], result[:])

@@ -37,12 +37,9 @@ def tile_fakematryoshkalinear_kernel(tc, x, code, scale, zero, bias, offs, out):
     ):
         scale_zero = held.tile([GROUPS, 2 * OUT], F32, name="scale_zero")
         nc.scalar.dma_start(scale_zero[:, 0:OUT], scale)
-        nc.scalar.dma_start(scale_zero[:, OUT : 2 * OUT], zero)
+        nc.sync.dma_start(scale_zero[:, OUT : 2 * OUT], zero)
         bias_rows = held.tile([P, OUT], F32, name="bias_rows")
         nc.scalar.dma_start(bias_rows[:], bias[0, :].partition_broadcast(P))
-
-        offsets = held.tile([P, PICKED // 16], U16, name="offsets")
-        nc.sync.dma_start(offsets[:], offs)
 
         code_sb = held.tile([P, PIECES, KTILES, OUT], BF16, name="code_sb")
         nc.sync.dma_start(code_sb[:], code.rearrange("(h p k) o -> p h k o", h=PIECES, k=KTILES))
@@ -52,9 +49,9 @@ def tile_fakematryoshkalinear_kernel(tc, x, code, scale, zero, bias, offs, out):
             x_block = windows.tile([P, FEATURES], F32, name="x_block")
             nc.sync.dma_start(x_block[:], x[b * P : (b + 1) * P, :])
             x_blocks.append(x_block)
-
-        identity = held.tile([P, P], F32, name="identity")
-        masks.make_identity(nc, identity[:])
+            if b == 0:
+                offsets = held.tile([P, PICKED // 16], U16, name="offsets")
+                nc.sync.dma_start(offsets[:], offs)
 
         selector = held.tile([GROUPS, PIECES * P], F32, name="selector")
         nc.gpsimd.memset(selector[:], 1.0)
@@ -66,24 +63,32 @@ def tile_fakematryoshkalinear_kernel(tc, x, code, scale, zero, bias, offs, out):
             out=selector[:], in_=selector[:], compare_op=alu.is_ge, fill=0.0,
             base=SHARE - 1, pattern=[[-1, PIECES * P]], channel_multiplier=SHARE,
         )
+        identity = held.tile([P, P], BF16, name="identity")
+        masks.make_identity(nc, identity[:])
 
         w = held.tile([P, PIECES, KTILES, OUT], BF16, name="w")
+        spreads = []
         for h in range(PIECES):
             spread = spread_banks.tile([P, 2 * OUT], F32, name="spread")
             nc.tensor.matmul(spread[:], selector[:, h * P : (h + 1) * P], scale_zero[:], start=True, stop=True)
+            spreads.append(spread)
+
+        def dequantise(h):
             shifted = work.tile([P, KTILES, OUT], F32, name="shifted")
             nc.vector.tensor_tensor(
                 shifted[:],
                 code_sb[:, h, :, :],
-                spread[:, OUT : 2 * OUT].unsqueeze(1).to_broadcast([P, KTILES, OUT]),
+                spreads[h][:, OUT : 2 * OUT].unsqueeze(1).to_broadcast([P, KTILES, OUT]),
                 alu.subtract,
             )
             nc.vector.tensor_tensor(
                 w[:, h, :, :],
                 shifted[:],
-                spread[:, 0:OUT].unsqueeze(1).to_broadcast([P, KTILES, OUT]),
+                spreads[h][:, 0:OUT].unsqueeze(1).to_broadcast([P, KTILES, OUT]),
                 alu.mult,
             )
+
+        dequantise(0)
 
         flipped_pieces = []
         sums = None
@@ -93,14 +98,18 @@ def tile_fakematryoshkalinear_kernel(tc, x, code, scale, zero, bias, offs, out):
                 picked = ring.tile([P, PIECE], F32, name="picked")
                 piece_offsets = offsets[:, h * (PIECE // 16) : (h + 1) * (PIECE // 16)]
                 nc.scalar.activation(picked[:], x_blocks[b][:].indirect(piece_offsets), copy)
+                picked_bf = ring.tile([P, PIECE], BF16, name="picked_bf")
+                nc.gpsimd.tensor_copy(picked_bf[:], picked[:])
 
-                by_tile = picked[:].rearrange("t (p k) -> t k p", k=KTILES)
-                flipped = flip_banks.tile([P, KTILES, P], F32, name="flipped")
+                by_tile = picked_bf[:].rearrange("t (p k) -> t k p", k=KTILES)
+                flipped = flip_banks.tile([P, KTILES, P], BF16, name="flipped")
                 for k in range(KTILES):
                     nc.tensor.transpose(flipped[:, k, :], by_tile[:, k, :], identity[:])
                 picked_t = ring.tile([P, KTILES, P], BF16, name="picked_t")
                 nc.vector.tensor_copy(picked_t[:], flipped[:])
                 flipped_pieces.append(picked_t)
+                if step + 1 < PIECES:
+                    dequantise(step + 1)
 
             if step > 0:
                 b, h = divmod(step - 1, PIECES)

@@ -42,7 +42,8 @@ def tile_fakematryoshkalinear_kernel(tc, x, code, scale, zero, bias, offs, out):
         nc.scalar.dma_start(bias_rows[:], bias[0, :].partition_broadcast(P))
 
         code_sb = held.tile([P, PIECES, KTILES, OUT], BF16, name="code_sb")
-        nc.sync.dma_start(code_sb[:], code.rearrange("(h p k) o -> p h k o", h=PIECES, k=KTILES))
+        code_pieces = code.rearrange("(h p k) o -> p h k o", h=PIECES, k=KTILES)
+        nc.sync.dma_start(code_sb[:, 0:1, :, :], code_pieces[:, 0:1, :, :])
 
         x_blocks = []
         for b in range(BLOCKS):
@@ -52,6 +53,7 @@ def tile_fakematryoshkalinear_kernel(tc, x, code, scale, zero, bias, offs, out):
             if b == 0:
                 offsets = held.tile([P, PICKED // 16], U16, name="offsets")
                 nc.sync.dma_start(offsets[:], offs)
+                nc.sync.dma_start(code_sb[:, 1:PIECES, :, :], code_pieces[:, 1:PIECES, :, :])
 
         selector = held.tile([GROUPS, PIECES * P], F32, name="selector")
         nc.gpsimd.memset(selector[:], 1.0)
@@ -63,7 +65,7 @@ def tile_fakematryoshkalinear_kernel(tc, x, code, scale, zero, bias, offs, out):
             out=selector[:], in_=selector[:], compare_op=alu.is_ge, fill=0.0,
             base=SHARE - 1, pattern=[[-1, PIECES * P]], channel_multiplier=SHARE,
         )
-        identity = held.tile([P, P], BF16, name="identity")
+        identity = held.tile([P, P], F32, name="identity")
         masks.make_identity(nc, identity[:])
 
         w = held.tile([P, PIECES, KTILES, OUT], BF16, name="w")
@@ -98,11 +100,9 @@ def tile_fakematryoshkalinear_kernel(tc, x, code, scale, zero, bias, offs, out):
                 picked = ring.tile([P, PIECE], F32, name="picked")
                 piece_offsets = offsets[:, h * (PIECE // 16) : (h + 1) * (PIECE // 16)]
                 nc.scalar.activation(picked[:], x_blocks[b][:].indirect(piece_offsets), copy)
-                picked_bf = ring.tile([P, PIECE], BF16, name="picked_bf")
-                nc.gpsimd.tensor_copy(picked_bf[:], picked[:])
 
-                by_tile = picked_bf[:].rearrange("t (p k) -> t k p", k=KTILES)
-                flipped = flip_banks.tile([P, KTILES, P], BF16, name="flipped")
+                by_tile = picked[:].rearrange("t (p k) -> t k p", k=KTILES)
+                flipped = flip_banks.tile([P, KTILES, P], F32, name="flipped")
                 for k in range(KTILES):
                     nc.tensor.transpose(flipped[:, k, :], by_tile[:, k, :], identity[:])
                 picked_t = ring.tile([P, KTILES, P], BF16, name="picked_t")

@@ -13,10 +13,12 @@ OUT = 256
 GROUP = 128
 GROUPS = PICKED // GROUP
 BLOCKS = TOKENS // P
-PIECE = 512
+PIECE = 1024
 PIECES = PICKED // PIECE
 KTILES = PIECE // P
 SHARE = P * GROUP // PIECE
+QUAD = 4
+QUADS = KTILES // QUAD
 
 FLOPS = 2 * TOKENS * PICKED * OUT
 
@@ -30,9 +32,9 @@ def tile_fakematryoshkalinear_kernel(tc, x, code, scale, zero, bias, offs, out):
         tc.tile_pool(name="held", bufs=1) as held,
         tc.tile_pool(name="windows", bufs=BLOCKS) as windows,
         tc.tile_pool(name="work", bufs=2) as work,
-        tc.tile_pool(name="ring", bufs=6) as ring,
+        tc.tile_pool(name="ring", bufs=4) as ring,
         tc.psum_pool(name="spread_banks", bufs=PIECES) as spread_banks,
-        tc.psum_pool(name="flip_banks", bufs=2) as flip_banks,
+        tc.psum_pool(name="flip_banks", bufs=4) as flip_banks,
         tc.psum_pool(name="sum_banks", bufs=2) as sum_banks,
     ):
         scale_zero = held.tile([GROUPS, 2 * OUT], F32, name="scale_zero")
@@ -42,8 +44,11 @@ def tile_fakematryoshkalinear_kernel(tc, x, code, scale, zero, bias, offs, out):
         nc.scalar.dma_start(bias_rows[:], bias[0, :].partition_broadcast(P))
 
         code_sb = held.tile([P, PIECES, KTILES, OUT], BF16, name="code_sb")
-        code_pieces = code.rearrange("(h p k) o -> p h k o", h=PIECES, k=KTILES)
-        nc.sync.dma_start(code_sb[:, 0:1, :, :], code_pieces[:, 0:1, :, :])
+        code_pieces = code.rearrange("(h p k) o -> h p k o", h=PIECES, k=KTILES)
+        nc.sync.dma_start(code_sb[:, 0, :, :], code_pieces[0])
+
+        offsets = held.tile([P, PICKED // 16], U16, name="offsets")
+        nc.sync.dma_start(offsets[:], offs)
 
         x_blocks = []
         for b in range(BLOCKS):
@@ -51,9 +56,8 @@ def tile_fakematryoshkalinear_kernel(tc, x, code, scale, zero, bias, offs, out):
             nc.sync.dma_start(x_block[:], x[b * P : (b + 1) * P, :])
             x_blocks.append(x_block)
             if b == 0:
-                offsets = held.tile([P, PICKED // 16], U16, name="offsets")
-                nc.sync.dma_start(offsets[:], offs)
-                nc.sync.dma_start(code_sb[:, 1:PIECES, :, :], code_pieces[:, 1:PIECES, :, :])
+                for h in range(1, PIECES):
+                    nc.sync.dma_start(code_sb[:, h, :, :], code_pieces[h])
 
         selector = held.tile([GROUPS, PIECES * P], F32, name="selector")
         nc.gpsimd.memset(selector[:], 1.0)
@@ -69,61 +73,49 @@ def tile_fakematryoshkalinear_kernel(tc, x, code, scale, zero, bias, offs, out):
         masks.make_identity(nc, identity[:])
 
         w = held.tile([P, PIECES, KTILES, OUT], BF16, name="w")
-        spreads = []
         for h in range(PIECES):
             spread = spread_banks.tile([P, 2 * OUT], F32, name="spread")
             nc.tensor.matmul(spread[:], selector[:, h * P : (h + 1) * P], scale_zero[:], start=True, stop=True)
-            spreads.append(spread)
+            for q in range(QUADS):
+                tiles = slice(q * QUAD, (q + 1) * QUAD)
+                shifted = work.tile([P, QUAD, OUT], F32, name="shifted")
+                nc.vector.tensor_tensor(
+                    shifted[:],
+                    code_sb[:, h, tiles, :],
+                    spread[:, OUT : 2 * OUT].unsqueeze(1).to_broadcast([P, QUAD, OUT]),
+                    alu.subtract,
+                )
+                nc.vector.tensor_tensor(
+                    w[:, h, tiles, :],
+                    shifted[:],
+                    spread[:, 0:OUT].unsqueeze(1).to_broadcast([P, QUAD, OUT]),
+                    alu.mult,
+                )
 
-        def dequantise(h):
-            shifted = work.tile([P, KTILES, OUT], F32, name="shifted")
-            nc.vector.tensor_tensor(
-                shifted[:],
-                code_sb[:, h, :, :],
-                spreads[h][:, OUT : 2 * OUT].unsqueeze(1).to_broadcast([P, KTILES, OUT]),
-                alu.subtract,
-            )
-            nc.vector.tensor_tensor(
-                w[:, h, :, :],
-                shifted[:],
-                spreads[h][:, 0:OUT].unsqueeze(1).to_broadcast([P, KTILES, OUT]),
-                alu.mult,
-            )
-
-        dequantise(0)
-
-        flipped_pieces = []
-        sums = None
-        for step in range(BLOCKS * PIECES + 1):
-            if step < BLOCKS * PIECES:
-                b, h = divmod(step, PIECES)
+        for b in range(BLOCKS):
+            sums = sum_banks.tile([P, OUT], F32, name="sums")
+            for h in range(PIECES):
                 picked = ring.tile([P, PIECE], F32, name="picked")
                 piece_offsets = offsets[:, h * (PIECE // 16) : (h + 1) * (PIECE // 16)]
                 nc.scalar.activation(picked[:], x_blocks[b][:].indirect(piece_offsets), copy)
 
                 by_tile = picked[:].rearrange("t (p k) -> t k p", k=KTILES)
-                flipped = flip_banks.tile([P, KTILES, P], F32, name="flipped")
-                for k in range(KTILES):
-                    nc.tensor.transpose(flipped[:, k, :], by_tile[:, k, :], identity[:])
                 picked_t = ring.tile([P, KTILES, P], BF16, name="picked_t")
-                nc.vector.tensor_copy(picked_t[:], flipped[:])
-                flipped_pieces.append(picked_t)
-                if step + 1 < PIECES:
-                    dequantise(step + 1)
+                for q in range(QUADS):
+                    flipped = flip_banks.tile([P, QUAD, P], F32, name="flipped")
+                    for i in range(QUAD):
+                        nc.tensor.transpose(flipped[:, i, :], by_tile[:, q * QUAD + i, :], identity[:])
+                    nc.vector.tensor_copy(picked_t[:, q * QUAD : (q + 1) * QUAD, :], flipped[:])
 
-            if step > 0:
-                b, h = divmod(step - 1, PIECES)
-                if h == 0:
-                    sums = sum_banks.tile([P, OUT], F32, name="sums")
                 for k in range(KTILES):
                     nc.tensor.matmul(
                         sums[:],
-                        flipped_pieces[step - 1][:, k, :],
+                        picked_t[:, k, :],
                         w[:, h, k, :],
                         start=(h == 0 and k == 0),
                         stop=(h == PIECES - 1 and k == KTILES - 1),
                     )
-                if h == PIECES - 1:
-                    result = work.tile([P, OUT], F32, name="result")
-                    nc.vector.tensor_tensor(result[:], sums[:], bias_rows[:], alu.add)
-                    nc.sync.dma_start(out[b * P : (b + 1) * P, :], result[:])
+
+            result = work.tile([P, OUT], F32, name="result")
+            nc.vector.tensor_tensor(result[:], sums[:], bias_rows[:], alu.add)
+            nc.sync.dma_start(out[b * P : (b + 1) * P, :], result[:])

@@ -13,12 +13,10 @@ OUT = 256
 GROUP = 128
 GROUPS = PICKED // GROUP
 BLOCKS = TOKENS // P
-PIECE = 1024
+PIECE = 512
 PIECES = PICKED // PIECE
 KTILES = PIECE // P
 SHARE = P * GROUP // PIECE
-QUAD = 4
-QUADS = KTILES // QUAD
 
 FLOPS = 2 * TOKENS * PICKED * OUT
 
@@ -32,9 +30,9 @@ def tile_fakematryoshkalinear_kernel(tc, x, code, scale, zero, bias, offs, out):
         tc.tile_pool(name="held", bufs=1) as held,
         tc.tile_pool(name="windows", bufs=BLOCKS) as windows,
         tc.tile_pool(name="work", bufs=2) as work,
-        tc.tile_pool(name="ring", bufs=4) as ring,
+        tc.tile_pool(name="ring", bufs=8) as ring,
         tc.psum_pool(name="spread_banks", bufs=PIECES) as spread_banks,
-        tc.psum_pool(name="flip_banks", bufs=4) as flip_banks,
+        tc.psum_pool(name="flip_banks", bufs=2) as flip_banks,
         tc.psum_pool(name="sum_banks", bufs=2) as sum_banks,
     ):
         scale_zero = held.tile([GROUPS, 2 * OUT], F32, name="scale_zero")
@@ -44,11 +42,8 @@ def tile_fakematryoshkalinear_kernel(tc, x, code, scale, zero, bias, offs, out):
         nc.scalar.dma_start(bias_rows[:], bias[0, :].partition_broadcast(P))
 
         code_sb = held.tile([P, PIECES, KTILES, OUT], BF16, name="code_sb")
-        code_pieces = code.rearrange("(h p k) o -> h p k o", h=PIECES, k=KTILES)
-        nc.sync.dma_start(code_sb[:, 0, :, :], code_pieces[0])
-
-        offsets = held.tile([P, PICKED // 16], U16, name="offsets")
-        nc.sync.dma_start(offsets[:], offs)
+        code_pieces = code.rearrange("(h p k) o -> p h k o", h=PIECES, k=KTILES)
+        nc.sync.dma_start(code_sb[:, 0:1, :, :], code_pieces[:, 0:1, :, :])
 
         x_blocks = []
         for b in range(BLOCKS):
@@ -56,8 +51,9 @@ def tile_fakematryoshkalinear_kernel(tc, x, code, scale, zero, bias, offs, out):
             nc.sync.dma_start(x_block[:], x[b * P : (b + 1) * P, :])
             x_blocks.append(x_block)
             if b == 0:
-                for h in range(1, PIECES):
-                    nc.sync.dma_start(code_sb[:, h, :, :], code_pieces[h])
+                offsets = held.tile([P, PICKED // 16], U16, name="offsets")
+                nc.sync.dma_start(offsets[:], offs)
+                nc.sync.dma_start(code_sb[:, 1:PIECES, :, :], code_pieces[:, 1:PIECES, :, :])
 
         selector = held.tile([GROUPS, PIECES * P], F32, name="selector")
         nc.gpsimd.memset(selector[:], 1.0)
@@ -73,49 +69,62 @@ def tile_fakematryoshkalinear_kernel(tc, x, code, scale, zero, bias, offs, out):
         masks.make_identity(nc, identity[:])
 
         w = held.tile([P, PIECES, KTILES, OUT], BF16, name="w")
+        spreads = []
         for h in range(PIECES):
             spread = spread_banks.tile([P, 2 * OUT], F32, name="spread")
             nc.tensor.matmul(spread[:], selector[:, h * P : (h + 1) * P], scale_zero[:], start=True, stop=True)
-            for q in range(QUADS):
-                tiles = slice(q * QUAD, (q + 1) * QUAD)
-                shifted = work.tile([P, QUAD, OUT], F32, name="shifted")
-                nc.vector.tensor_tensor(
-                    shifted[:],
-                    code_sb[:, h, tiles, :],
-                    spread[:, OUT : 2 * OUT].unsqueeze(1).to_broadcast([P, QUAD, OUT]),
-                    alu.subtract,
-                )
-                nc.vector.tensor_tensor(
-                    w[:, h, tiles, :],
-                    shifted[:],
-                    spread[:, 0:OUT].unsqueeze(1).to_broadcast([P, QUAD, OUT]),
-                    alu.mult,
-                )
+            spreads.append(spread)
 
-        for b in range(BLOCKS):
-            sums = sum_banks.tile([P, OUT], F32, name="sums")
-            for h in range(PIECES):
+        def dequantise(h):
+            shifted = work.tile([P, KTILES, OUT], F32, name="shifted")
+            nc.vector.tensor_tensor(
+                shifted[:],
+                code_sb[:, h, :, :],
+                spreads[h][:, OUT : 2 * OUT].unsqueeze(1).to_broadcast([P, KTILES, OUT]),
+                alu.subtract,
+            )
+            nc.vector.tensor_tensor(
+                w[:, h, :, :],
+                shifted[:],
+                spreads[h][:, 0:OUT].unsqueeze(1).to_broadcast([P, KTILES, OUT]),
+                alu.mult,
+            )
+
+        dequantise(0)
+        dequantise(1)
+
+        flipped_pieces = []
+        sums = None
+        for step in range(BLOCKS * PIECES + 1):
+            if step < BLOCKS * PIECES:
+                b, h = divmod(step, PIECES)
                 picked = ring.tile([P, PIECE], F32, name="picked")
                 piece_offsets = offsets[:, h * (PIECE // 16) : (h + 1) * (PIECE // 16)]
                 nc.scalar.activation(picked[:], x_blocks[b][:].indirect(piece_offsets), copy)
 
                 by_tile = picked[:].rearrange("t (p k) -> t k p", k=KTILES)
+                flipped = flip_banks.tile([P, KTILES, P], F32, name="flipped")
+                for k in range(KTILES):
+                    nc.tensor.transpose(flipped[:, k, :], by_tile[:, k, :], identity[:])
                 picked_t = ring.tile([P, KTILES, P], BF16, name="picked_t")
-                for q in range(QUADS):
-                    flipped = flip_banks.tile([P, QUAD, P], F32, name="flipped")
-                    for i in range(QUAD):
-                        nc.tensor.transpose(flipped[:, i, :], by_tile[:, q * QUAD + i, :], identity[:])
-                    nc.vector.tensor_copy(picked_t[:, q * QUAD : (q + 1) * QUAD, :], flipped[:])
+                nc.vector.tensor_copy(picked_t[:], flipped[:])
+                flipped_pieces.append(picked_t)
+                if step + 2 < PIECES:
+                    dequantise(step + 2)
 
+            if step > 0:
+                b, h = divmod(step - 1, PIECES)
+                if h == 0:
+                    sums = sum_banks.tile([P, OUT], F32, name="sums")
                 for k in range(KTILES):
                     nc.tensor.matmul(
                         sums[:],
-                        picked_t[:, k, :],
+                        flipped_pieces[step - 1][:, k, :],
                         w[:, h, k, :],
                         start=(h == 0 and k == 0),
                         stop=(h == PIECES - 1 and k == KTILES - 1),
                     )
-
-            result = work.tile([P, OUT], F32, name="result")
-            nc.vector.tensor_tensor(result[:], sums[:], bias_rows[:], alu.add)
-            nc.sync.dma_start(out[b * P : (b + 1) * P, :], result[:])
+                if h == PIECES - 1:
+                    result = work.tile([P, OUT], F32, name="result")
+                    nc.vector.tensor_tensor(result[:], sums[:], bias_rows[:], alu.add)
+                    nc.sync.dma_start(out[b * P : (b + 1) * P, :], result[:])

@@ -103,11 +103,19 @@ def tile_fakematryoshkalinear_kernel(tc, x, code, scale, zero, bias, offs, out):
                 nc.scalar.activation(picked[:], x_blocks[b][:].indirect(piece_offsets), copy)
 
                 by_tile = picked[:].rearrange("t (p k) -> t k p", k=KTILES)
-                flipped = flip_banks.tile([P, KTILES, P], F32, name="flipped")
-                for k in range(KTILES):
-                    nc.tensor.transpose(flipped[:, k, :], by_tile[:, k, :], identity[:])
                 picked_t = ring.tile([P, KTILES, P], BF16, name="picked_t")
-                nc.vector.tensor_copy(picked_t[:], flipped[:])
+                if step < BLOCKS * PIECES - 1:
+                    flipped = flip_banks.tile([P, KTILES, P], F32, name="flipped")
+                    for k in range(KTILES):
+                        nc.tensor.transpose(flipped[:, k, :], by_tile[:, k, :], identity[:])
+                    nc.vector.tensor_copy(picked_t[:], flipped[:])
+                else:
+                    half = KTILES // 2
+                    for first, rounder in ((0, nc.vector.tensor_copy), (half, nc.scalar.copy)):
+                        flipped = flip_banks.tile([P, KTILES, P], F32, name="flipped")
+                        for k in range(half):
+                            nc.tensor.transpose(flipped[:, k, :], by_tile[:, first + k, :], identity[:])
+                        rounder(picked_t[:, first : first + half, :], flipped[:, 0:half, :])
                 flipped_pieces.append(picked_t)
                 if step + 2 < PIECES:
                     dequantise(step + 2)

@@ -37,23 +37,23 @@ def tile_fakematryoshkalinear_kernel(tc, x, code, scale, zero, bias, offs, out):
     ):
         scale_zero = held.tile([GROUPS, 2 * OUT], F32, name="scale_zero")
         nc.scalar.dma_start(scale_zero[:, 0:OUT], scale)
-        nc.sync.dma_start(scale_zero[:, OUT : 2 * OUT], zero)
-        bias_rows = held.tile([P, OUT], F32, name="bias_rows")
-        nc.scalar.dma_start(bias_rows[:], bias[0, :].partition_broadcast(P))
+        nc.scalar.dma_start(scale_zero[:, OUT : 2 * OUT], zero)
+        offsets = held.tile([P, PICKED // 16], U16, name="offsets")
+        nc.sync.dma_start(offsets[:], offs)
 
         code_sb = held.tile([P, PIECES, KTILES, OUT], BF16, name="code_sb")
         code_pieces = code.rearrange("(h p k) o -> p h k o", h=PIECES, k=KTILES)
-        nc.sync.dma_start(code_sb[:, 0:1, :, :], code_pieces[:, 0:1, :, :])
+        bias_rows = held.tile([P, OUT], F32, name="bias_rows")
 
         x_blocks = []
         for b in range(BLOCKS):
             x_block = windows.tile([P, FEATURES], F32, name="x_block")
             nc.sync.dma_start(x_block[:], x[b * P : (b + 1) * P, :])
             x_blocks.append(x_block)
-            if b == 0:
-                offsets = held.tile([P, PICKED // 16], U16, name="offsets")
-                nc.sync.dma_start(offsets[:], offs)
-                nc.sync.dma_start(code_sb[:, 1:PIECES, :, :], code_pieces[:, 1:PIECES, :, :])
+            if b < 2:
+                nc.sync.dma_start(code_sb[:, 2 * b : 2 * b + 2, :, :], code_pieces[:, 2 * b : 2 * b + 2, :, :])
+            if b == 1:
+                nc.sync.dma_start(bias_rows[:], bias[0, :].partition_broadcast(P))
 
         selector = held.tile([GROUPS, PIECES * P], F32, name="selector")
         nc.gpsimd.memset(selector[:], 1.0)

@@ -37,7 +37,7 @@ def tile_fakematryoshkalinear_kernel(tc, x, code, scale, zero, bias, offs, out):
     ):
         scale_zero = held.tile([GROUPS, 2 * OUT], F32, name="scale_zero")
         nc.scalar.dma_start(scale_zero[:, 0:OUT], scale)
-        nc.scalar.dma_start(scale_zero[:, OUT : 2 * OUT], zero)
+        nc.sync.dma_start(scale_zero[:, OUT : 2 * OUT], zero)
         offsets = held.tile([P, PICKED // 16], U16, name="offsets")
         nc.sync.dma_start(offsets[:], offs)
 

@@ -52,7 +52,7 @@ def tile_fakematryoshkalinear_kernel(tc, x, code, scale, zero, bias, offs, out):
             x_blocks.append(x_block)
             if b < 2:
                 nc.sync.dma_start(code_sb[:, 2 * b : 2 * b + 2, :, :], code_pieces[:, 2 * b : 2 * b + 2, :, :])
-            if b == 1:
+            if b == 2:
                 nc.sync.dma_start(bias_rows[:], bias[0, :].partition_broadcast(P))
 
         selector = held.tile([GROUPS, PIECES * P], F32, name="selector")

@@ -65,7 +65,7 @@ def tile_fakematryoshkalinear_kernel(tc, x, code, scale, zero, bias, offs, out):
             out=selector[:], in_=selector[:], compare_op=alu.is_ge, fill=0.0,
             base=SHARE - 1, pattern=[[-1, PIECES * P]], channel_multiplier=SHARE,
         )
-        identity = held.tile([P, P], F32, name="identity")
+        identity = held.tile([P, P], BF16, name="identity")
         masks.make_identity(nc, identity[:])
 
         w = held.tile([P, PIECES, KTILES, OUT], BF16, name="w")
@@ -102,20 +102,26 @@ def tile_fakematryoshkalinear_kernel(tc, x, code, scale, zero, bias, offs, out):
                 piece_offsets = offsets[:, h * (PIECE // 16) : (h + 1) * (PIECE // 16)]
                 nc.scalar.activation(picked[:], x_blocks[b][:].indirect(piece_offsets), copy)
 
-                by_tile = picked[:].rearrange("t (p k) -> t k p", k=KTILES)
+                rounded = ring.tile([P, PIECE], BF16, name="rounded")
+                if step < BLOCKS * PIECES - 1:
+                    nc.gpsimd.tensor_scalar(rounded[:], picked[:], 1.0, 0.0, alu.mult, alu.add)
+                else:
+                    nc.vector.tensor_copy(rounded[:], picked[:])
+
+                by_tile = rounded[:].rearrange("t (p k) -> t k p", k=KTILES)
                 picked_t = ring.tile([P, KTILES, P], BF16, name="picked_t")
                 if step < BLOCKS * PIECES - 1:
-                    flipped = flip_banks.tile([P, KTILES, P], F32, name="flipped")
+                    flipped = flip_banks.tile([P, KTILES, P], BF16, name="flipped")
                     for k in range(KTILES):
                         nc.tensor.transpose(flipped[:, k, :], by_tile[:, k, :], identity[:])
                     nc.vector.tensor_copy(picked_t[:], flipped[:])
                 else:
                     half = KTILES // 2
-                    for first, rounder in ((0, nc.vector.tensor_copy), (half, nc.scalar.copy)):
-                        flipped = flip_banks.tile([P, KTILES, P], F32, name="flipped")
+                    for first, move in ((0, nc.vector.tensor_copy), (half, nc.scalar.copy)):
+                        flipped = flip_banks.tile([P, KTILES, P], BF16, name="flipped")
                         for k in range(half):
                             nc.tensor.transpose(flipped[:, k, :], by_tile[:, first + k, :], identity[:])
-                        rounder(picked_t[:, first : first + half, :], flipped[:, 0:half, :])
+                        move(picked_t[:, first : first + half, :], flipped[:, 0:half, :])
                 flipped_pieces.append(picked_t)
                 if step + 2 < PIECES:
                     dequantise(step + 2)

@@ -15,6 +15,7 @@ GROUPS = PICKED // GROUP
 BLOCKS = TOKENS // P
 PIECE = 512
 PIECES = PICKED // PIECE
+LATE = PIECES - 1
 KTILES = PIECE // P
 SHARE = P * GROUP // PIECE
 
@@ -31,9 +32,10 @@ def tile_fakematryoshkalinear_kernel(tc, x, code, scale, zero, bias, offs, out):
         tc.tile_pool(name="windows", bufs=BLOCKS) as windows,
         tc.tile_pool(name="work", bufs=2) as work,
         tc.tile_pool(name="ring", bufs=8) as ring,
-        tc.psum_pool(name="spread_banks", bufs=PIECES) as spread_banks,
+        tc.tile_pool(name="kept", bufs=BLOCKS) as kept,
+        tc.psum_pool(name="spread_banks", bufs=2) as spread_banks,
         tc.psum_pool(name="flip_banks", bufs=2) as flip_banks,
-        tc.psum_pool(name="sum_banks", bufs=2) as sum_banks,
+        tc.psum_pool(name="sum_banks", bufs=BLOCKS) as sum_banks,
     ):
         scale_zero = held.tile([GROUPS, 2 * OUT], F32, name="scale_zero")
         nc.scalar.dma_start(scale_zero[:, 0:OUT], scale)
@@ -45,15 +47,20 @@ def tile_fakematryoshkalinear_kernel(tc, x, code, scale, zero, bias, offs, out):
         code_pieces = code.rearrange("(h p k) o -> p h k o", h=PIECES, k=KTILES)
         bias_rows = held.tile([P, OUT], F32, name="bias_rows")
 
+        def load_codes(first, end):
+            nc.sync.dma_start(code_sb[:, first:end, :, :], code_pieces[:, first:end, :, :])
+
         x_blocks = []
         for b in range(BLOCKS):
             x_block = windows.tile([P, FEATURES], F32, name="x_block")
             nc.sync.dma_start(x_block[:], x[b * P : (b + 1) * P, :])
             x_blocks.append(x_block)
-            if b < 2:
-                nc.sync.dma_start(code_sb[:, 2 * b : 2 * b + 2, :, :], code_pieces[:, 2 * b : 2 * b + 2, :, :])
-            if b == 2:
-                nc.sync.dma_start(bias_rows[:], bias[0, :].partition_broadcast(P))
+            if b == 0:
+                load_codes(0, 2)
+            if b == 1:
+                load_codes(2, LATE)
+        load_codes(LATE, PIECES)
+        nc.sync.dma_start(bias_rows[:], bias[0, :].partition_broadcast(P))
 
         selector = held.tile([GROUPS, PIECES * P], F32, name="selector")
         nc.gpsimd.memset(selector[:], 1.0)
@@ -69,11 +76,12 @@ def tile_fakematryoshkalinear_kernel(tc, x, code, scale, zero, bias, offs, out):
         masks.make_identity(nc, identity[:])
 
         w = held.tile([P, PIECES, KTILES, OUT], BF16, name="w")
-        spreads = []
-        for h in range(PIECES):
+        spreads = {}
+
+        def spread_rows(h):
             spread = spread_banks.tile([P, 2 * OUT], F32, name="spread")
             nc.tensor.matmul(spread[:], selector[:, h * P : (h + 1) * P], scale_zero[:], start=True, stop=True)
-            spreads.append(spread)
+            spreads[h] = spread
 
         def dequantise(h):
             shifted = work.tile([P, KTILES, OUT], F32, name="shifted")
@@ -90,55 +98,74 @@ def tile_fakematryoshkalinear_kernel(tc, x, code, scale, zero, bias, offs, out):
                 alu.mult,
             )
 
+        flipped_pieces = {}
+        sums = []
+
+        def multiply(b, h):
+            if h == 0:
+                sums.append(sum_banks.tile([P, OUT], F32, name="sums"))
+            for k in range(KTILES):
+                nc.tensor.matmul(
+                    sums[b][:],
+                    flipped_pieces[b, h][:, k, :],
+                    w[:, h, k, :],
+                    start=(h == 0 and k == 0),
+                    stop=(h == LATE and k == KTILES - 1),
+                )
+            if h == LATE:
+                result = work.tile([P, OUT], F32, name="result")
+                nc.vector.tensor_tensor(result[:], sums[b][:], bias_rows[:], alu.add)
+                nc.sync.dma_start(out[b * P : (b + 1) * P, :], result[:])
+
+        spread_rows(0)
+        spread_rows(1)
         dequantise(0)
-        dequantise(1)
+        steps = [(b, h) for b in range(BLOCKS) for h in range(PIECES)]
+        for step, (b, h) in enumerate(steps):
+            picked = ring.tile([P, PIECE], F32, name="picked")
+            piece_offsets = offsets[:, h * (PIECE // 16) : (h + 1) * (PIECE // 16)]
+            nc.scalar.activation(picked[:], x_blocks[b][:].indirect(piece_offsets), copy)
 
-        flipped_pieces = []
-        sums = None
-        for step in range(BLOCKS * PIECES + 1):
-            if step < BLOCKS * PIECES:
-                b, h = divmod(step, PIECES)
-                picked = ring.tile([P, PIECE], F32, name="picked")
-                piece_offsets = offsets[:, h * (PIECE // 16) : (h + 1) * (PIECE // 16)]
-                nc.scalar.activation(picked[:], x_blocks[b][:].indirect(piece_offsets), copy)
+            rounded = ring.tile([P, PIECE], BF16, name="rounded")
+            if step < len(steps) - 1:
+                nc.gpsimd.tensor_scalar(rounded[:], picked[:], 1.0, 0.0, alu.mult, alu.add)
+            else:
+                nc.vector.tensor_copy(rounded[:], picked[:])
 
-                rounded = ring.tile([P, PIECE], BF16, name="rounded")
-                if step < BLOCKS * PIECES - 1:
-                    nc.gpsimd.tensor_scalar(rounded[:], picked[:], 1.0, 0.0, alu.mult, alu.add)
-                else:
-                    nc.vector.tensor_copy(rounded[:], picked[:])
-
-                by_tile = rounded[:].rearrange("t (p k) -> t k p", k=KTILES)
+            by_tile = rounded[:].rearrange("t (p k) -> t k p", k=KTILES)
+            if h >= 2:
+                picked_t = kept.tile([P, KTILES, P], BF16, name=f"picked_t{h}")
+            else:
                 picked_t = ring.tile([P, KTILES, P], BF16, name="picked_t")
-                if step < BLOCKS * PIECES - 1:
+            flipped_pieces[b, h] = picked_t
+            if step < len(steps) - 1:
+                flipped = flip_banks.tile([P, KTILES, P], BF16, name="flipped")
+                for k in range(KTILES):
+                    nc.tensor.transpose(flipped[:, k, :], by_tile[:, k, :], identity[:])
+                nc.vector.tensor_copy(picked_t[:], flipped[:])
+            else:
+                half = KTILES // 2
+                for first, move in ((0, nc.vector.tensor_copy), (half, nc.scalar.copy)):
                     flipped = flip_banks.tile([P, KTILES, P], BF16, name="flipped")
-                    for k in range(KTILES):
-                        nc.tensor.transpose(flipped[:, k, :], by_tile[:, k, :], identity[:])
-                    nc.vector.tensor_copy(picked_t[:], flipped[:])
-                else:
-                    half = KTILES // 2
-                    for first, move in ((0, nc.vector.tensor_copy), (half, nc.scalar.copy)):
-                        flipped = flip_banks.tile([P, KTILES, P], BF16, name="flipped")
-                        for k in range(half):
-                            nc.tensor.transpose(flipped[:, k, :], by_tile[:, first + k, :], identity[:])
-                        move(picked_t[:, first : first + half, :], flipped[:, 0:half, :])
-                flipped_pieces.append(picked_t)
-                if step + 2 < PIECES:
-                    dequantise(step + 2)
+                    for k in range(half):
+                        nc.tensor.transpose(flipped[:, k, :], by_tile[:, first + k, :], identity[:])
+                    move(picked_t[:, first : first + half, :], flipped[:, 0:half, :])
+
+            if (b, h) == (0, 0):
+                dequantise(1)
+                spread_rows(2)
+            if (b, h) == (1, 1):
+                dequantise(2)
+                spread_rows(LATE)
+            if (b, h) == (BLOCKS - 1, 0):
+                dequantise(LATE)
 
             if step > 0:
-                b, h = divmod(step - 1, PIECES)
-                if h == 0:
-                    sums = sum_banks.tile([P, OUT], F32, name="sums")
-                for k in range(KTILES):
-                    nc.tensor.matmul(
-                        sums[:],
-                        flipped_pieces[step - 1][:, k, :],
-                        w[:, h, k, :],
-                        start=(h == 0 and k == 0),
-                        stop=(h == PIECES - 1 and k == KTILES - 1),
-                    )
-                if h == PIECES - 1:
-                    result = work.tile([P, OUT], F32, name="result")
-                    nc.vector.tensor_tensor(result[:], sums[:], bias_rows[:], alu.add)
-                    nc.sync.dma_start(out[b * P : (b + 1) * P, :], result[:])
+                before_b, before_h = steps[step - 1]
+                if before_h < LATE and (before_b, before_h) != (0, 2):
+                    multiply(before_b, before_h)
+                if (before_b, before_h) == (1, 2):
+                    multiply(0, 2)
+            if b == BLOCKS - 1 and h > 0:
+                multiply(h - 1, LATE)
+        multiply(BLOCKS - 1, LATE)

@@ -17,6 +17,7 @@ PIECE = 512
 PIECES = PICKED // PIECE
 LATE = PIECES - 1
 KTILES = PIECE // P
+PAIRS = KTILES // 2
 SHARE = P * GROUP // PIECE
 
 FLOPS = 2 * TOKENS * PICKED * OUT
@@ -59,7 +60,8 @@ def tile_fakematryoshkalinear_kernel(tc, x, code, scale, zero, bias, offs, out):
                 load_codes(0, 2)
             if b == 1:
                 load_codes(2, LATE)
-        load_codes(LATE, PIECES)
+            if b == 2:
+                load_codes(LATE, PIECES)
         nc.sync.dma_start(bias_rows[:], bias[0, :].partition_broadcast(P))
 
         selector = held.tile([GROUPS, PIECES * P], F32, name="selector")
@@ -72,7 +74,7 @@ def tile_fakematryoshkalinear_kernel(tc, x, code, scale, zero, bias, offs, out):
             out=selector[:], in_=selector[:], compare_op=alu.is_ge, fill=0.0,
             base=SHARE - 1, pattern=[[-1, PIECES * P]], channel_multiplier=SHARE,
         )
-        identity = held.tile([P, P], BF16, name="identity")
+        identity = held.tile([P, P], F32, name="identity")
         masks.make_identity(nc, identity[:])
 
         w = held.tile([P, PIECES, KTILES, OUT], BF16, name="w")
@@ -104,18 +106,20 @@ def tile_fakematryoshkalinear_kernel(tc, x, code, scale, zero, bias, offs, out):
         def multiply(b, h):
             if h == 0:
                 sums.append(sum_banks.tile([P, OUT], F32, name="sums"))
+            by_tile = flipped_pieces[b, h][:].bitcast(BF16).rearrange("p q (t u) -> p q u t", u=2)
             for k in range(KTILES):
                 nc.tensor.matmul(
                     sums[b][:],
-                    flipped_pieces[b, h][:, k, :],
+                    by_tile[:, k // 2, k % 2, :],
                     w[:, h, k, :],
                     start=(h == 0 and k == 0),
                     stop=(h == LATE and k == KTILES - 1),
                 )
-            if h == LATE:
-                result = work.tile([P, OUT], F32, name="result")
-                nc.vector.tensor_tensor(result[:], sums[b][:], bias_rows[:], alu.add)
-                nc.sync.dma_start(out[b * P : (b + 1) * P, :], result[:])
+
+        def finish(b):
+            result = work.tile([P, OUT], F32, name="result")
+            nc.vector.tensor_tensor(result[:], sums[b][:], bias_rows[:], alu.add)
+            nc.sync.dma_start(out[b * P : (b + 1) * P, :], result[:])
 
         spread_rows(0)
         spread_rows(1)
@@ -132,24 +136,18 @@ def tile_fakematryoshkalinear_kernel(tc, x, code, scale, zero, bias, offs, out):
             else:
                 nc.vector.tensor_copy(rounded[:], picked[:])
 
-            by_tile = rounded[:].rearrange("t (p k) -> t k p", k=KTILES)
+            words = rounded[:].bitcast(F32).rearrange("t (p q) -> t q p", q=PAIRS)
             if h >= 2:
-                picked_t = kept.tile([P, KTILES, P], BF16, name=f"picked_t{h}")
+                picked_t = kept.tile([P, PAIRS, P], F32, name=f"picked_t{h}")
             else:
-                picked_t = ring.tile([P, KTILES, P], BF16, name="picked_t")
+                picked_t = ring.tile([P, PAIRS, P], F32, name="picked_t")
             flipped_pieces[b, h] = picked_t
-            if step < len(steps) - 1:
-                flipped = flip_banks.tile([P, KTILES, P], BF16, name="flipped")
-                for k in range(KTILES):
-                    nc.tensor.transpose(flipped[:, k, :], by_tile[:, k, :], identity[:])
-                nc.vector.tensor_copy(picked_t[:], flipped[:])
-            else:
-                half = KTILES // 2
-                for first, move in ((0, nc.vector.tensor_copy), (half, nc.scalar.copy)):
-                    flipped = flip_banks.tile([P, KTILES, P], BF16, name="flipped")
-                    for k in range(half):
-                        nc.tensor.transpose(flipped[:, k, :], by_tile[:, first + k, :], identity[:])
-                    move(picked_t[:, first : first + half, :], flipped[:, 0:half, :])
+            flipped = flip_banks.tile([P, PAIRS, P], F32, name="flipped")
+            for q in range(PAIRS):
+                nc.tensor.transpose(flipped[:, q, :], words[:, q, :], identity[:])
+            if (b, h) == (BLOCKS - 1, 0):
+                dequantise(LATE)
+            nc.vector.tensor_copy(picked_t[:], flipped[:])
 
             if (b, h) == (0, 0):
                 dequantise(1)
@@ -157,8 +155,6 @@ def tile_fakematryoshkalinear_kernel(tc, x, code, scale, zero, bias, offs, out):
             if (b, h) == (1, 1):
                 dequantise(2)
                 spread_rows(LATE)
-            if (b, h) == (BLOCKS - 1, 0):
-                dequantise(LATE)
 
             if step > 0:
                 before_b, before_h = steps[step - 1]
@@ -166,6 +162,10 @@ def tile_fakematryoshkalinear_kernel(tc, x, code, scale, zero, bias, offs, out):
                     multiply(before_b, before_h)
                 if (before_b, before_h) == (1, 2):
                     multiply(0, 2)
+            if b == BLOCKS - 1 and h > 1:
+                finish(h - 2)
             if b == BLOCKS - 1 and h > 0:
                 multiply(h - 1, LATE)
         multiply(BLOCKS - 1, LATE)
+        finish(BLOCKS - 2)
+        finish(BLOCKS - 1)

@@ -17,7 +17,6 @@ PIECE = 512
 PIECES = PICKED // PIECE
 LATE = PIECES - 1
 KTILES = PIECE // P
-PAIRS = KTILES // 2
 SHARE = P * GROUP // PIECE
 
 FLOPS = 2 * TOKENS * PICKED * OUT
@@ -46,7 +45,6 @@ def tile_fakematryoshkalinear_kernel(tc, x, code, scale, zero, bias, offs, out):
 
         code_sb = held.tile([P, PIECES, KTILES, OUT], BF16, name="code_sb")
         code_pieces = code.rearrange("(h p k) o -> p h k o", h=PIECES, k=KTILES)
-        bias_rows = held.tile([P, OUT], F32, name="bias_rows")
 
         def load_codes(first, end):
             nc.sync.dma_start(code_sb[:, first:end, :, :], code_pieces[:, first:end, :, :])
@@ -60,9 +58,10 @@ def tile_fakematryoshkalinear_kernel(tc, x, code, scale, zero, bias, offs, out):
                 load_codes(0, 2)
             if b == 1:
                 load_codes(2, LATE)
+                bias_row = held.tile([1, OUT], F32, name="bias_row")
+                nc.sync.dma_start(bias_row[:], bias)
             if b == 2:
                 load_codes(LATE, PIECES)
-        nc.sync.dma_start(bias_rows[:], bias[0, :].partition_broadcast(P))
 
         selector = held.tile([GROUPS, PIECES * P], F32, name="selector")
         nc.gpsimd.memset(selector[:], 1.0)
@@ -74,16 +73,20 @@ def tile_fakematryoshkalinear_kernel(tc, x, code, scale, zero, bias, offs, out):
             out=selector[:], in_=selector[:], compare_op=alu.is_ge, fill=0.0,
             base=SHARE - 1, pattern=[[-1, PIECES * P]], channel_multiplier=SHARE,
         )
-        identity = held.tile([P, P], F32, name="identity")
+        identity = held.tile([P, P], BF16, name="identity")
         masks.make_identity(nc, identity[:])
 
         w = held.tile([P, PIECES, KTILES, OUT], BF16, name="w")
         spreads = {}
-
-        def spread_rows(h):
+        for h in (2, 3, 0, 1):
             spread = spread_banks.tile([P, 2 * OUT], F32, name="spread")
             nc.tensor.matmul(spread[:], selector[:, h * P : (h + 1) * P], scale_zero[:], start=True, stop=True)
-            spreads[h] = spread
+            if h < 2:
+                spreads[h] = spread
+            else:
+                spread_sb = held.tile([P, 2 * OUT], F32, name=f"spread_sb{h}")
+                nc.vector.tensor_copy(spread_sb[:], spread[:])
+                spreads[h] = spread_sb
 
         def dequantise(h):
             shifted = work.tile([P, KTILES, OUT], F32, name="shifted")
@@ -100,17 +103,19 @@ def tile_fakematryoshkalinear_kernel(tc, x, code, scale, zero, bias, offs, out):
                 alu.mult,
             )
 
+        ones = held.tile([1, P], F32, name="ones")
+        nc.gpsimd.memset(ones[:], 1.0)
+        bias_rows = held.tile([P, OUT], F32, name="bias_rows")
         flipped_pieces = {}
         sums = []
 
         def multiply(b, h):
             if h == 0:
                 sums.append(sum_banks.tile([P, OUT], F32, name="sums"))
-            by_tile = flipped_pieces[b, h][:].bitcast(BF16).rearrange("p q (t u) -> p q u t", u=2)
             for k in range(KTILES):
                 nc.tensor.matmul(
                     sums[b][:],
-                    by_tile[:, k // 2, k % 2, :],
+                    flipped_pieces[b, h][:, k, :],
                     w[:, h, k, :],
                     start=(h == 0 and k == 0),
                     stop=(h == LATE and k == KTILES - 1),
@@ -121,8 +126,6 @@ def tile_fakematryoshkalinear_kernel(tc, x, code, scale, zero, bias, offs, out):
             nc.vector.tensor_tensor(result[:], sums[b][:], bias_rows[:], alu.add)
             nc.sync.dma_start(out[b * P : (b + 1) * P, :], result[:])
 
-        spread_rows(0)
-        spread_rows(1)
         dequantise(0)
         steps = [(b, h) for b in range(BLOCKS) for h in range(PIECES)]
         for step, (b, h) in enumerate(steps):
@@ -131,41 +134,55 @@ def tile_fakematryoshkalinear_kernel(tc, x, code, scale, zero, bias, offs, out):
             nc.scalar.activation(picked[:], x_blocks[b][:].indirect(piece_offsets), copy)
 
             rounded = ring.tile([P, PIECE], BF16, name="rounded")
-            if step < len(steps) - 1:
+            if b < BLOCKS - 1:
                 nc.gpsimd.tensor_scalar(rounded[:], picked[:], 1.0, 0.0, alu.mult, alu.add)
             else:
                 nc.vector.tensor_copy(rounded[:], picked[:])
 
-            words = rounded[:].bitcast(F32).rearrange("t (p q) -> t q p", q=PAIRS)
+            by_tile = rounded[:].rearrange("t (p k) -> t k p", k=KTILES)
             if h >= 2:
-                picked_t = kept.tile([P, PAIRS, P], F32, name=f"picked_t{h}")
+                picked_t = kept.tile([P, KTILES, P], BF16, name=f"picked_t{h}")
             else:
-                picked_t = ring.tile([P, PAIRS, P], F32, name="picked_t")
+                picked_t = ring.tile([P, KTILES, P], BF16, name="picked_t")
             flipped_pieces[b, h] = picked_t
-            flipped = flip_banks.tile([P, PAIRS, P], F32, name="flipped")
-            for q in range(PAIRS):
-                nc.tensor.transpose(flipped[:, q, :], words[:, q, :], identity[:])
-            if (b, h) == (BLOCKS - 1, 0):
-                dequantise(LATE)
-            nc.vector.tensor_copy(picked_t[:], flipped[:])
+            if step < len(steps) - 1:
+                flipped = flip_banks.tile([P, KTILES, P], BF16, name="flipped")
+                for k in range(KTILES):
+                    nc.tensor.transpose(flipped[:, k, :], by_tile[:, k, :], identity[:])
+                nc.vector.tensor_copy(picked_t[:], flipped[:])
+            else:
+                half = KTILES // 2
+                for first, move in ((0, nc.vector.tensor_copy), (half, nc.scalar.copy)):
+                    flipped = flip_banks.tile([P, half, P], BF16, name="flipped")
+                    for k in range(half):
+                        nc.tensor.transpose(flipped[:, k, :], by_tile[:, first + k, :], identity[:])
+                    move(picked_t[:, first : first + half, :], flipped[:])
 
             if (b, h) == (0, 0):
                 dequantise(1)
-                spread_rows(2)
             if (b, h) == (1, 1):
                 dequantise(2)
-                spread_rows(LATE)
+            if (b, h) == (2, 0):
+                dequantise(LATE)
+            if (b, h) == (2, 1):
+                bias_sum = sum_banks.tile([P, OUT], F32, name="sums")
+                nc.tensor.matmul(bias_sum[:], ones[:], bias_row[:], start=True, stop=True)
+                nc.vector.tensor_copy(bias_rows[:], bias_sum[:])
 
             if step > 0:
-                before_b, before_h = steps[step - 1]
-                if before_h < LATE and (before_b, before_h) != (0, 2):
-                    multiply(before_b, before_h)
-                if (before_b, before_h) == (1, 2):
+                before = steps[step - 1]
+                if before not in ((0, 2), (0, LATE), (1, LATE)):
+                    multiply(*before)
+                if before == (1, 2):
                     multiply(0, 2)
-            if b == BLOCKS - 1 and h > 1:
-                finish(h - 2)
-            if b == BLOCKS - 1 and h > 0:
-                multiply(h - 1, LATE)
+                if before == (2, 2):
+                    multiply(0, LATE)
+                if before == (2, LATE):
+                    multiply(1, LATE)
+            if (b, h) == (3, 0):
+                finish(0)
+            if (b, h) == (3, 1):
+                finish(2)
+                finish(1)
         multiply(BLOCKS - 1, LATE)
-        finish(BLOCKS - 2)
         finish(BLOCKS - 1)

@@ -17,6 +17,7 @@ PIECE = 512
 PIECES = PICKED // PIECE
 LATE = PIECES - 1
 KTILES = PIECE // P
+PAIRS = KTILES // 2
 SHARE = P * GROUP // PIECE
 
 FLOPS = 2 * TOKENS * PICKED * OUT
@@ -73,7 +74,7 @@ def tile_fakematryoshkalinear_kernel(tc, x, code, scale, zero, bias, offs, out):
             out=selector[:], in_=selector[:], compare_op=alu.is_ge, fill=0.0,
             base=SHARE - 1, pattern=[[-1, PIECES * P]], channel_multiplier=SHARE,
         )
-        identity = held.tile([P, P], BF16, name="identity")
+        identity = held.tile([P, P], F32, name="identity")
         masks.make_identity(nc, identity[:])
 
         w = held.tile([P, PIECES, KTILES, OUT], BF16, name="w")
@@ -106,8 +107,41 @@ def tile_fakematryoshkalinear_kernel(tc, x, code, scale, zero, bias, offs, out):
         ones = held.tile([1, P], F32, name="ones")
         nc.gpsimd.memset(ones[:], 1.0)
         bias_rows = held.tile([P, OUT], F32, name="bias_rows")
-        flipped_pieces = {}
+        tiles = {}
         sums = []
+
+        def tiles_of(picked_t):
+            by_tile = picked_t[:].bitcast(BF16).rearrange("p q (t u) -> p q u t", u=2)
+            return [by_tile[:, k // 2, k % 2, :] for k in range(KTILES)]
+
+        def round_and_flip(picked, b, h):
+            rounded = ring.tile([P, PIECE], BF16, name="rounded")
+            if b < BLOCKS - 1:
+                nc.gpsimd.tensor_scalar(rounded[:], picked[:], 1.0, 0.0, alu.mult, alu.add)
+            else:
+                nc.vector.tensor_copy(rounded[:], picked[:])
+            words = rounded[:].bitcast(F32).rearrange("t (p q) -> t q p", q=PAIRS)
+            flipped = flip_banks.tile([P, PAIRS, P], F32, name="flipped")
+            for q in range(PAIRS):
+                nc.tensor.transpose(flipped[:, q, :], words[:, q, :], identity[:])
+            if h >= 2:
+                picked_t = kept.tile([P, PAIRS, P], F32, name=f"picked_t{h}")
+            else:
+                picked_t = ring.tile([P, PAIRS, P], F32, name="picked_t")
+            nc.vector.tensor_copy(picked_t[:], flipped[:])
+            return tiles_of(picked_t)
+
+        def round_and_flip_last(picked):
+            by_pair = picked[:].rearrange("t (p q u) -> t q p u", q=PAIRS, u=2)
+            rounded = held.tile([P, PAIRS, 2 * P], BF16, name="last_rounded")
+            picked_t = held.tile([P, PAIRS, P], F32, name="last_picked_t")
+            for q in range(PAIRS):
+                nc.scalar.copy(rounded[:, q, :].rearrange("t (p u) -> t p u", u=2), by_pair[:, q, :, :])
+            for q, move in ((0, nc.vector.tensor_copy), (1, nc.scalar.copy)):
+                flipped = flip_banks.tile([P, P], F32, name="flipped")
+                nc.tensor.transpose(flipped[:], rounded[:, q, :].bitcast(F32), identity[:])
+                move(picked_t[:, q, :], flipped[:])
+            return tiles_of(picked_t)
 
         def multiply(b, h):
             if h == 0:
@@ -115,7 +149,7 @@ def tile_fakematryoshkalinear_kernel(tc, x, code, scale, zero, bias, offs, out):
             for k in range(KTILES):
                 nc.tensor.matmul(
                     sums[b][:],
-                    flipped_pieces[b, h][:, k, :],
+                    tiles[b, h][k],
                     w[:, h, k, :],
                     start=(h == 0 and k == 0),
                     stop=(h == LATE and k == KTILES - 1),
@@ -133,30 +167,10 @@ def tile_fakematryoshkalinear_kernel(tc, x, code, scale, zero, bias, offs, out):
             piece_offsets = offsets[:, h * (PIECE // 16) : (h + 1) * (PIECE // 16)]
             nc.scalar.activation(picked[:], x_blocks[b][:].indirect(piece_offsets), copy)
 
-            rounded = ring.tile([P, PIECE], BF16, name="rounded")
-            if b < BLOCKS - 1:
-                nc.gpsimd.tensor_scalar(rounded[:], picked[:], 1.0, 0.0, alu.mult, alu.add)
-            else:
-                nc.vector.tensor_copy(rounded[:], picked[:])
-
-            by_tile = rounded[:].rearrange("t (p k) -> t k p", k=KTILES)
-            if h >= 2:
-                picked_t = kept.tile([P, KTILES, P], BF16, name=f"picked_t{h}")
-            else:
-                picked_t = ring.tile([P, KTILES, P], BF16, name="picked_t")
-            flipped_pieces[b, h] = picked_t
             if step < len(steps) - 1:
-                flipped = flip_banks.tile([P, KTILES, P], BF16, name="flipped")
-                for k in range(KTILES):
-                    nc.tensor.transpose(flipped[:, k, :], by_tile[:, k, :], identity[:])
-                nc.vector.tensor_copy(picked_t[:], flipped[:])
+                tiles[b, h] = round_and_flip(picked, b, h)
             else:
-                half = KTILES // 2
-                for first, move in ((0, nc.vector.tensor_copy), (half, nc.scalar.copy)):
-                    flipped = flip_banks.tile([P, half, P], BF16, name="flipped")
-                    for k in range(half):
-                        nc.tensor.transpose(flipped[:, k, :], by_tile[:, first + k, :], identity[:])
-                    move(picked_t[:, first : first + half, :], flipped[:])
+                tiles[b, h] = round_and_flip_last(picked)
 
             if (b, h) == (0, 0):
                 dequantise(1)

import concourse.masks as masks
import concourse.mybir as mybir

F32 = mybir.dt.float32
BF16 = mybir.dt.bfloat16
U16 = mybir.dt.uint16

P = 128
TOKENS = 512
FEATURES = 4096
PICKED = 2048
OUT = 256
GROUP = 128
GROUPS = PICKED // GROUP
BLOCKS = TOKENS // P
PIECE = 512
PIECES = PICKED // PIECE
LATE = PIECES - 1
KTILES = PIECE // P
PAIRS = KTILES // 2
SHARE = P * GROUP // PIECE

FLOPS = 2 * TOKENS * PICKED * OUT


def tile_fakematryoshkalinear_kernel(tc, x, code, scale, zero, bias, offs, out):
    nc = tc.nc
    copy = mybir.ActivationFunctionType.Copy
    alu = mybir.AluOpType

    with (
        tc.tile_pool(name="held", bufs=1) as held,
        tc.tile_pool(name="windows", bufs=BLOCKS) as windows,
        tc.tile_pool(name="work", bufs=2) as work,
        tc.tile_pool(name="ring", bufs=8) as ring,
        tc.tile_pool(name="kept", bufs=BLOCKS) as kept,
        tc.psum_pool(name="spread_banks", bufs=2) as spread_banks,
        tc.psum_pool(name="flip_banks", bufs=2) as flip_banks,
        tc.psum_pool(name="sum_banks", bufs=BLOCKS) as sum_banks,
    ):
        scale_zero = held.tile([GROUPS, 2 * OUT], F32, name="scale_zero")
        nc.scalar.dma_start(scale_zero[:, 0:OUT], scale)
        nc.sync.dma_start(scale_zero[:, OUT : 2 * OUT], zero)
        offsets = held.tile([P, PICKED // 16], U16, name="offsets")
        nc.sync.dma_start(offsets[:], offs)

        code_sb = held.tile([P, PIECES, KTILES, OUT], BF16, name="code_sb")
        code_pieces = code.rearrange("(h p k) o -> p h k o", h=PIECES, k=KTILES)

        def load_codes(first, end):
            nc.sync.dma_start(code_sb[:, first:end, :, :], code_pieces[:, first:end, :, :])

        x_blocks = []
        for b in range(BLOCKS):
            x_block = windows.tile([P, FEATURES], F32, name="x_block")
            nc.sync.dma_start(x_block[:], x[b * P : (b + 1) * P, :])
            x_blocks.append(x_block)
            if b == 0:
                load_codes(0, 2)
            if b == 1:
                load_codes(2, LATE)
                bias_row = held.tile([1, OUT], F32, name="bias_row")
                nc.sync.dma_start(bias_row[:], bias)
            if b == 2:
                load_codes(LATE, PIECES)

        selector = held.tile([GROUPS, PIECES * P], F32, name="selector")
        nc.gpsimd.memset(selector[:], 1.0)
        nc.gpsimd.affine_select(
            out=selector[:], in_=selector[:], compare_op=alu.is_ge, fill=0.0,
            base=0, pattern=[[1, PIECES * P]], channel_multiplier=-SHARE,
        )
        nc.gpsimd.affine_select(
            out=selector[:], in_=selector[:], compare_op=alu.is_ge, fill=0.0,
            base=SHARE - 1, pattern=[[-1, PIECES * P]], channel_multiplier=SHARE,
        )
        identity = held.tile([P, P], F32, name="identity")
        masks.make_identity(nc, identity[:])

        w = held.tile([P, PIECES, KTILES, OUT], BF16, name="w")
        spreads = {}
        for h in (2, 3, 0, 1):
            spread = spread_banks.tile([P, 2 * OUT], F32, name="spread")
            nc.tensor.matmul(spread[:], selector[:, h * P : (h + 1) * P], scale_zero[:], start=True, stop=True)
            if h < 2:
                spreads[h] = spread
            else:
                spread_sb = held.tile([P, 2 * OUT], F32, name=f"spread_sb{h}")
                nc.vector.tensor_copy(spread_sb[:], spread[:])
                spreads[h] = spread_sb

        def dequantise(h):
            shifted = work.tile([P, KTILES, OUT], F32, name="shifted")
            nc.vector.tensor_tensor(
                shifted[:],
                code_sb[:, h, :, :],
                spreads[h][:, OUT : 2 * OUT].unsqueeze(1).to_broadcast([P, KTILES, OUT]),
                alu.subtract,
            )
            nc.vector.tensor_tensor(
                w[:, h, :, :],
                shifted[:],
                spreads[h][:, 0:OUT].unsqueeze(1).to_broadcast([P, KTILES, OUT]),
                alu.mult,
            )

        ones = held.tile([1, P], F32, name="ones")
        nc.gpsimd.memset(ones[:], 1.0)
        bias_rows = held.tile([P, OUT], F32, name="bias_rows")
        tiles = {}
        sums = []

        def tiles_of(picked_t):
            by_tile = picked_t[:].bitcast(BF16).rearrange("p q (t u) -> p q u t", u=2)
            return [by_tile[:, k // 2, k % 2, :] for k in range(KTILES)]

        def round_and_flip(picked, b, h):
            rounded = ring.tile([P, PIECE], BF16, name="rounded")
            if b < BLOCKS - 1:
                nc.gpsimd.tensor_scalar(rounded[:], picked[:], 1.0, 0.0, alu.mult, alu.add)
            else:
                nc.vector.tensor_copy(rounded[:], picked[:])
            words = rounded[:].bitcast(F32).rearrange("t (p q) -> t q p", q=PAIRS)
            flipped = flip_banks.tile([P, PAIRS, P], F32, name="flipped")
            for q in range(PAIRS):
                nc.tensor.transpose(flipped[:, q, :], words[:, q, :], identity[:])
            if h >= 2:
                picked_t = kept.tile([P, PAIRS, P], F32, name=f"picked_t{h}")
            else:
                picked_t = ring.tile([P, PAIRS, P], F32, name="picked_t")
            nc.vector.tensor_copy(picked_t[:], flipped[:])
            return tiles_of(picked_t)

        def round_and_flip_last(picked):
            by_pair = picked[:].rearrange("t (p q u) -> t q p u", q=PAIRS, u=2)
            rounded = held.tile([P, PAIRS, 2 * P], BF16, name="last_rounded")
            picked_t = held.tile([P, PAIRS, P], F32, name="last_picked_t")
            for q in range(PAIRS):
                nc.scalar.copy(rounded[:, q, :].rearrange("t (p u) -> t p u", u=2), by_pair[:, q, :, :])
            for q, move in ((0, nc.vector.tensor_copy), (1, nc.scalar.copy)):
                flipped = flip_banks.tile([P, P], F32, name="flipped")
                nc.tensor.transpose(flipped[:], rounded[:, q, :].bitcast(F32), identity[:])
                move(picked_t[:, q, :], flipped[:])
            return tiles_of(picked_t)

        def multiply(b, h):
            if h == 0:
                sums.append(sum_banks.tile([P, OUT], F32, name="sums"))
            for k in range(KTILES):
                nc.tensor.matmul(
                    sums[b][:],
                    tiles[b, h][k],
                    w[:, h, k, :],
                    start=(h == 0 and k == 0),
                    stop=(h == LATE and k == KTILES - 1),
                )

        def finish(b):
            result = work.tile([P, OUT], F32, name="result")
            nc.vector.tensor_tensor(result[:], sums[b][:], bias_rows[:], alu.add)
            nc.sync.dma_start(out[b * P : (b + 1) * P, :], result[:])

        dequantise(0)
        steps = [(b, h) for b in range(BLOCKS) for h in range(PIECES)]
        for step, (b, h) in enumerate(steps):
            picked = ring.tile([P, PIECE], F32, name="picked")
            piece_offsets = offsets[:, h * (PIECE // 16) : (h + 1) * (PIECE // 16)]
            nc.scalar.activation(picked[:], x_blocks[b][:].indirect(piece_offsets), copy)

            if step < len(steps) - 1:
                tiles[b, h] = round_and_flip(picked, b, h)
            else:
                tiles[b, h] = round_and_flip_last(picked)

            if (b, h) == (0, 0):
                dequantise(1)
            if (b, h) == (1, 1):
                dequantise(2)
            if (b, h) == (2, 0):
                dequantise(LATE)
            if (b, h) == (2, 1):
                bias_sum = sum_banks.tile([P, OUT], F32, name="sums")
                nc.tensor.matmul(bias_sum[:], ones[:], bias_row[:], start=True, stop=True)
                nc.vector.tensor_copy(bias_rows[:], bias_sum[:])

            if step > 0:
                before = steps[step - 1]
                if before not in ((0, 2), (0, LATE), (1, LATE)):
                    multiply(*before)
                if before == (1, 2):
                    multiply(0, 2)
                if before == (2, 2):
                    multiply(0, LATE)
                if before == (2, LATE):
                    multiply(1, LATE)
            if (b, h) == (3, 0):
                finish(0)
            if (b, h) == (3, 1):
                finish(2)
                finish(1)
        multiply(BLOCKS - 1, LATE)
        finish(BLOCKS - 1)
